import numpy as np
import ml_dtypes


def mxq(x, axis, fmt="e4m3"):
    dtype, down = {"e4m3": (ml_dtypes.float8_e4m3fn, 7), "e5m2": (ml_dtypes.float8_e5m2, 14)}[fmt]
    v = np.moveaxis(np.asarray(x, np.float32).astype(ml_dtypes.bfloat16).astype(np.float64), axis, -1)
    blocks = v.reshape(v.shape[:-1] + (-1, 32))
    amax = np.abs(blocks).max(-1, keepdims=True)
    byte = np.maximum(np.where(amax > 0, np.frexp(amax)[1] - 1 + 127, 0) - down, 1)
    scale = np.exp2(byte - 127.0)
    codes = (blocks / scale).astype(np.float32).astype(dtype).astype(np.float64)
    return np.moveaxis((codes * scale).reshape(v.shape), -1, axis)


WIDE = False


def mx_kscale(k):
    if not WIDE:
        return np.ones(k)
    levels = np.array([10, -10, 5, -5, 0])
    if k % 512:
        return np.exp2(np.random.permutation(np.resize(levels, k // 32))).repeat(32)
    a = np.empty((k // 512, 16))
    for p in range(k // 512):
        a[p, :8] = np.random.permutation(np.resize(levels, 8))
        for g in range(8):
            far = levels[np.abs(levels - a[p, g]) >= 10]
            a[p, g + 8] = far[np.random.randint(len(far))]
    return np.exp2(a.ravel()).repeat(32)


BF16 = ml_dtypes.bfloat16


def bf(x):
    return np.asarray(x, np.float32).astype(BF16)


def f64(x):
    return np.asarray(x).astype(np.float64)


L, N, E, H, C, LW, RW = 8192, 1, 512, 8, 512, 1, 1
EPS = 1e-8


def sigmoid(v):
    return 1.0 / (1.0 + np.exp(-v))


def setup_inputs():
    s = mx_kscale(E)
    return {"attn_out": bf(np.random.standard_normal((L, N, E)) * 2.0),
            "norm_scale": bf((1.0 + 0.1 * np.random.standard_normal(E)) * s),
            "norm_gate": bf(1.0 + 0.2 * np.random.standard_normal(E)),
            "w_o": bf(np.random.standard_normal((E, E)) / np.sqrt(E) / s[None, :]),
            "b_o": bf(np.random.standard_normal(E) * 0.1)}


def reference(attn_out, norm_scale, norm_gate, w_o, b_o):
    x = f64(attn_out)
    rms = np.sqrt(np.mean(x * x, axis=-1, keepdims=True))
    y = f64(norm_scale) * (x / (rms + EPS)) * sigmoid(f64(norm_gate) * x)
    return (mxq(y, 2, "e4m3") @ mxq(f64(w_o), 1, "e4m3").T) + f64(b_o)

@@ -1,0 +1,250 @@
+from contextlib import ExitStack
+import math
+
+import concourse.mybir as mybir
+from concourse.masks import make_identity
+
+FLOPS = 2 * 8192 * 512 * 512
+
+BF16 = mybir.dt.bfloat16
+F32 = mybir.dt.float32
+U32 = mybir.dt.uint32
+U8 = mybir.dt.uint8
+FP8X4 = mybir.dt.float8_e4m3fn_x4
+ACT = mybir.ActivationFunctionType
+ALU = mybir.AluOpType
+
+P = 128
+PACK = 4
+FEATURES = P * PACK
+OUT_FEATURES = 512
+TILES = 4
+GROUP = TILES * P
+VECTOR_SUMS = 2
+EPS = 1e-8
+GATE_FLOOR = 2.0**-64
+
+
+def tile_normlocalattention_pb_t_kernel(tc, attn_out, norm_scale, norm_gate, w_o, b_o, out):
+    nc = tc.nc
+    x_rows = attn_out.flatten_outer_dims()
+    out_rows = out.flatten_outer_dims()
+    groups = x_rows.shape[0] // GROUP
+
+    def rows_of_group(rows, g):
+        return rows[g * GROUP : (g + 1) * GROUP, :].rearrange("(p j) k -> p j k", j=TILES)
+
+    with ExitStack() as stack:
+        stack.enter_context(tc.manual_schedule())
+        const = stack.enter_context(tc.tile_pool(name="const", bufs=1))
+        x_pool = stack.enter_context(tc.tile_pool(name="x", bufs=1))
+        stats = stack.enter_context(tc.tile_pool(name="stats", bufs=4))
+        work = stack.enter_context(tc.tile_pool(name="work", bufs=3))
+        single = stack.enter_context(tc.tile_pool(name="single", bufs=1))
+        results = stack.enter_context(tc.tile_pool(name="results", bufs=3))
+        psum_words = stack.enter_context(tc.psum_pool(name="psum_words", bufs=3))
+        psum_inv = stack.enter_context(tc.psum_pool(name="psum_inv", bufs=1))
+        psum_acc = stack.enter_context(tc.psum_pool(name="psum_acc", bufs=TILES))
+
+        gate_bf = const.tile([P, PACK], BF16)
+        scale_bf = const.tile([P, PACK], BF16)
+        nc.scalar.dma_start(out=gate_bf[:], in_=norm_gate.rearrange("(p t) -> p t", t=PACK))
+        nc.scalar.dma_start(out=scale_bf[:], in_=norm_scale.rearrange("(p t) -> p t", t=PACK))
+        x_tiles = [x_pool.tile([P, TILES, FEATURES], BF16, name="x_tile_%d" % g) for g in range(groups)]
+        w_rows = const.tile([P, OUT_FEATURES // P, FEATURES], BF16)
+        bias = const.tile([P, OUT_FEATURES], BF16)
+        for j in range(TILES):
+            nc.sync.dma_start(out=x_tiles[0][:, j, :], in_=rows_of_group(x_rows, 0)[:, j, :])
+        nc.sync.dma_start(out=x_tiles[1][:], in_=rows_of_group(x_rows, 1))
+        nc.sync.dma_start(out=w_rows[:], in_=w_o.rearrange("(c p) k -> p c k", p=P))
+        nc.sync.dma_start(out=x_tiles[2][:], in_=rows_of_group(x_rows, 2))
+        nc.sync.dma_start(out=bias[:], in_=b_o.partition_broadcast(P))
+        for g in range(3, groups):
+            nc.sync.dma_start(out=x_tiles[g][:], in_=rows_of_group(x_rows, g))
+
+        ident = const.tile([P, P], F32)
+        make_identity(nc, ident[:])
+        half = const.tile([P, TILES], F32)
+        nc.vector.memset(half[:], 0.5)
+        warm = const.tile([P, 1], F32)
+        nc.scalar.activation(out=warm[:], in_=half[:, 0:1], func=ACT.Silu)
+
+        gate = const.tile([P, PACK], F32)
+        size = const.tile([P, PACK], F32)
+        lift = const.tile([P, PACK], F32)
+        gain = const.tile([P, PACK], F32)
+        nc.vector.tensor_copy(out=gate[:], in_=gate_bf[:])
+        nc.vector.tensor_scalar_mul(out=size[:], in0=gate[:], scalar1=-1.0)
+        nc.vector.tensor_max(out=size[:], in0=size[:], in1=gate[:])
+        nc.vector.tensor_scalar(
+            out=lift[:], in0=size[:], scalar1=GATE_FLOOR, scalar2=GATE_FLOOR, op0=ALU.is_lt, op1=ALU.mult
+        )
+        nc.vector.tensor_add(out=gate[:], in0=gate[:], in1=lift[:])
+        nc.vector.reciprocal(out=gain[:], in_=gate[:])
+        nc.vector.tensor_mul(out=gain[:], in0=gain[:], in1=scale_bf[:])
+
+        w_codes = const.tile([P, OUT_FEATURES], U32, align_bytes=64)
+        w_scales = const.tile([P, OUT_FEATURES], U8, align_bytes=64)
+
+        def prepare_weights():
+            w_grouped = const.tile([P, OUT_FEATURES, 2], F32, align_bytes=64)
+            for h in range(2):
+                w_words = psum_acc.tile([P, 2, 2 * P], F32, name="w_words", tag="acc")
+                for u in range(2):
+                    for c in range(2):
+                        nc.tensor.transpose(
+                            w_words[:, u, c * P : (c + 1) * P],
+                            w_rows[:, 2 * h + c, :].bitcast(F32)[:, u : 2 * P : 2],
+                            ident[:],
+                        )
+                nc.vector.tensor_copy(
+                    out=w_grouped[:, h * 2 * P : (h + 1) * 2 * P, :],
+                    in_=w_words[:].rearrange("p u o -> p o u"),
+                )
+            nc.vector.quantize_mx(
+                out=w_codes[:].bitcast(FP8X4),
+                scales=w_scales[:],
+                in_=w_grouped[:].rearrange("p o u -> p (o u)").bitcast(BF16),
+            )
+
+        rms_of = {}
+        inv_all_of = {}
+        x_words_of = {}
+        silu_of = {}
+        y_planes_of = {}
+        y_grouped_of = {}
+        y_codes_of = {}
+        y_scales_of = {}
+        acc_of = {}
+
+        def root_mean_squares(g):
+            squares = work.tile([P, TILES, FEATURES], BF16, name="squares")
+            mean_sq = stats.tile([P, TILES], F32, name="mean_sq")
+            for j in range(TILES):
+                if g < VECTOR_SUMS:
+                    nc.vector.scalar_tensor_tensor(
+                        out=squares[:, j, :],
+                        in0=x_tiles[g][:, j, :],
+                        scalar=1.0 / FEATURES,
+                        in1=x_tiles[g][:, j, :],
+                        op0=ALU.mult,
+                        op1=ALU.mult,
+                        accum_out=mean_sq[:, j : j + 1],
+                    )
+                else:
+                    nc.scalar.activation(
+                        out=squares[:, j, :],
+                        in_=x_tiles[g][:, j, :],
+                        func=ACT.Square,
+                        scale=1.0 / math.sqrt(FEATURES),
+                        accum_out=mean_sq[:, j : j + 1],
+                    )
+            rms = stats.tile([P, TILES], F32, name="rms")
+            nc.gpsimd.tensor_tensor(out=rms[:], in0=mean_sq[:], in1=half[:], op=ALU.pow)
+            nc.gpsimd.tensor_scalar(out=rms[:], in0=rms[:], scalar1=EPS, scalar2=1.0, op0=ALU.add, op1=ALU.mult)
+            rms_of[g] = rms
+
+        def spread_inverse_rms(g):
+            inv = stats.tile([P, TILES], F32, name="inv")
+            nc.vector.reciprocal(out=inv[:], in_=rms_of[g][:])
+            inv_all = psum_inv.tile([P, GROUP], F32, name="inv_all")
+            for j in range(TILES):
+                nc.tensor.transpose(
+                    inv_all[:, j * P : (j + 1) * P], inv[:, j : j + 1].to_broadcast([P, P]), ident[:]
+                )
+            inv_all_of[g] = inv_all
+
+        def transpose_x(g):
+            for u in range(2):
+                x_words = psum_words.tile([P, GROUP], F32, name="x_words")
+                for j in range(TILES):
+                    nc.tensor.transpose(
+                        x_words[:, j * P : (j + 1) * P],
+                        x_tiles[g][:, j, :].bitcast(F32)[:, u : 2 * P : 2],
+                        ident[:],
+                    )
+                x_words_of[(g, u)] = x_words
+
+        def gated(g):
+            silu = work.tile([P, PACK, GROUP], F32, name="silu")
+            for u in range(2):
+                pairs = x_words_of[(g, u)][:].bitcast(BF16).rearrange("p (m e) -> p m e", e=2)
+                for e in range(2):
+                    t = 2 * u + e
+                    nc.scalar.activation(
+                        out=silu[:, t, :], in_=pairs[:, :, e], func=ACT.Silu, scale=gate[:, t : t + 1]
+                    )
+            silu_of[g] = silu
+
+        def normed(g):
+            y_planes = work.tile([P, PACK, GROUP], BF16, name="y_planes")
+            for t in range(PACK):
+                nc.vector.scalar_tensor_tensor(
+                    out=y_planes[:, t, :],
+                    in0=silu_of[g][:, t, :],
+                    scalar=gain[:, t : t + 1],
+                    in1=inv_all_of[g][:],
+                    op0=ALU.mult,
+                    op1=ALU.mult,
+                )
+            y_planes_of[g] = y_planes
+
+        def regroup(g):
+            y_grouped = single.tile([P, GROUP, PACK], BF16, name="y_grouped", align_bytes=64)
+            nc.gpsimd.tensor_scalar(
+                out=y_grouped[:],
+                in0=y_planes_of[g][:].rearrange("p t m -> p m t"),
+                scalar1=1.0,
+                scalar2=0.0,
+                op0=ALU.mult,
+                op1=ALU.add,
+            )
+            y_grouped_of[g] = y_grouped
+
+        def quantise(g):
+            y_codes = work.tile([P, GROUP], U32, name="y_codes", align_bytes=64)
+            y_scales = work.tile([P, GROUP], U8, name="y_scales", align_bytes=64)
+            nc.vector.quantize_mx(
+                out=y_codes[:].bitcast(FP8X4),
+                scales=y_scales[:],
+                in_=y_grouped_of[g][:].rearrange("p m t -> p (m t)"),
+            )
+            y_codes_of[g] = y_codes
+            y_scales_of[g] = y_scales
+
+        def multiply(g):
+            for j in range(TILES):
+                acc = psum_acc.tile([P, OUT_FEATURES], F32, name="acc")
+                nc.tensor.matmul_mx(
+                    out=acc[:],
+                    lhsT=y_codes_of[g][:, j * P : (j + 1) * P].bitcast(FP8X4),
+                    lhsT_scale=y_scales_of[g][:, j * P : (j + 1) * P],
+                    rhs=w_codes[:].bitcast(FP8X4),
+                    rhs_scale=w_scales[:],
+                    start=True,
+                    stop=True,
+                )
+                acc_of[(g, j)] = acc
+
+        def add_bias_and_store(g):
+            result = results.tile([P, TILES, OUT_FEATURES], F32, name="result")
+            for j in range(TILES):
+                nc.vector.tensor_tensor(out=result[:, j, :], in0=acc_of[(g, j)][:], in1=bias[:], op=ALU.add)
+                nc.sync.dma_start(out=rows_of_group(out_rows, g)[:, j, :], in_=result[:, j, :])
+
+        def run(stage, g):
+            if 0 <= g < groups:
+                stage(g)
+
+        for step in range(-2, groups + 2):
+            run(gated, step + 1)
+            run(transpose_x, step + 2)
+            run(root_mean_squares, step + 2)
+            run(normed, step)
+            run(spread_inverse_rms, step + 1)
+            if step == 0:
+                prepare_weights()
+            run(quantise, step - 1)
+            run(multiply, step - 1)
+            run(add_bias_and_store, step - 2)
+            run(regroup, step)

@@ -20,7 +20,8 @@ FEATURES = P * PACK
 OUT_FEATURES = 512
 TILES = 4
 GROUP = TILES * P
-VECTOR_SUMS = 2
+RUN = 4
+VECTOR_SUMS = [(0, 0), (0, 1), (1, 0), (1, 1), (1, 2), (1, 3)]
 EPS = 1e-8
 GATE_FLOOR = 2.0**-64
 
@@ -40,31 +41,30 @@ def tile_normlocalattention_pb_t_kernel(tc, attn_out, norm_scale, norm_gate, w_o
         x_pool = stack.enter_context(tc.tile_pool(name="x", bufs=1))
         stats = stack.enter_context(tc.tile_pool(name="stats", bufs=4))
         work = stack.enter_context(tc.tile_pool(name="work", bufs=3))
-        single = stack.enter_context(tc.tile_pool(name="single", bufs=1))
+        factors = stack.enter_context(tc.tile_pool(name="factors", bufs=2 * TILES))
         results = stack.enter_context(tc.tile_pool(name="results", bufs=3))
-        psum_words = stack.enter_context(tc.psum_pool(name="psum_words", bufs=3))
-        psum_inv = stack.enter_context(tc.psum_pool(name="psum_inv", bufs=1))
+        psum_words = stack.enter_context(tc.psum_pool(name="psum_words", bufs=2))
+        psum_factor = stack.enter_context(tc.psum_pool(name="psum_factor", bufs=2))
         psum_acc = stack.enter_context(tc.psum_pool(name="psum_acc", bufs=TILES))
 
         gate_bf = const.tile([P, PACK], BF16)
         scale_bf = const.tile([P, PACK], BF16)
+        bias_bf = const.tile([P, PACK], BF16)
         nc.scalar.dma_start(out=gate_bf[:], in_=norm_gate.rearrange("(p t) -> p t", t=PACK))
         nc.scalar.dma_start(out=scale_bf[:], in_=norm_scale.rearrange("(p t) -> p t", t=PACK))
+        nc.scalar.dma_start(out=bias_bf[:], in_=b_o.rearrange("(p t) -> p t", t=PACK))
         x_tiles = [x_pool.tile([P, TILES, FEATURES], BF16, name="x_tile_%d" % g) for g in range(groups)]
         w_rows = const.tile([P, OUT_FEATURES // P, FEATURES], BF16)
-        bias = const.tile([P, OUT_FEATURES], BF16)
         for j in range(TILES):
             nc.sync.dma_start(out=x_tiles[0][:, j, :], in_=rows_of_group(x_rows, 0)[:, j, :])
         nc.sync.dma_start(out=x_tiles[1][:], in_=rows_of_group(x_rows, 1))
         nc.sync.dma_start(out=w_rows[:], in_=w_o.rearrange("(c p) k -> p c k", p=P))
-        nc.sync.dma_start(out=x_tiles[2][:], in_=rows_of_group(x_rows, 2))
-        nc.sync.dma_start(out=bias[:], in_=b_o.partition_broadcast(P))
-        for g in range(3, groups):
+        for g in range(2, groups):
             nc.sync.dma_start(out=x_tiles[g][:], in_=rows_of_group(x_rows, g))
 
         ident = const.tile([P, P], F32)
         make_identity(nc, ident[:])
-        half = const.tile([P, TILES], F32)
+        half = const.tile([P, 2 * TILES], F32)
         nc.vector.memset(half[:], 0.5)
         warm = const.tile([P, 1], F32)
         nc.scalar.activation(out=warm[:], in_=half[:, 0:1], func=ACT.Silu)
@@ -73,147 +73,172 @@ def tile_normlocalattention_pb_t_kernel(tc, attn_out, norm_scale, norm_gate, w_o
         size = const.tile([P, PACK], F32)
         lift = const.tile([P, PACK], F32)
         gain = const.tile([P, PACK], F32)
-        nc.vector.tensor_copy(out=gate[:], in_=gate_bf[:])
-        nc.vector.tensor_scalar_mul(out=size[:], in0=gate[:], scalar1=-1.0)
-        nc.vector.tensor_max(out=size[:], in0=size[:], in1=gate[:])
+        bias = const.tile([P, PACK], F32)
+        nc.vector.scalar_tensor_tensor(
+            out=size[:], in0=gate_bf[:], scalar=-1.0, in1=gate_bf[:], op0=ALU.mult, op1=ALU.max
+        )
         nc.vector.tensor_scalar(
             out=lift[:], in0=size[:], scalar1=GATE_FLOOR, scalar2=GATE_FLOOR, op0=ALU.is_lt, op1=ALU.mult
         )
-        nc.vector.tensor_add(out=gate[:], in0=gate[:], in1=lift[:])
-        nc.vector.reciprocal(out=gain[:], in_=gate[:])
-        nc.vector.tensor_mul(out=gain[:], in0=gain[:], in1=scale_bf[:])
+        nc.vector.tensor_add(out=gate[:], in0=gate_bf[:], in1=lift[:])
 
+        gain_row = const.tile([P, PACK, P], F32)
+        bias_row = const.tile([P, P, PACK], F32)
+
+        def spread(column_tile):
+            rows = psum_acc.tile([P, PACK, P], F32, name="rows", tag="acc")
+            for t in range(PACK):
+                nc.tensor.transpose(rows[:, t, :], column_tile[:, t : t + 1].to_broadcast([P, P]), ident[:])
+            return rows
+
+        w_grouped = const.tile([P, OUT_FEATURES, 2], F32, align_bytes=64)
         w_codes = const.tile([P, OUT_FEATURES], U32, align_bytes=64)
         w_scales = const.tile([P, OUT_FEATURES], U8, align_bytes=64)
 
-        def prepare_weights():
-            w_grouped = const.tile([P, OUT_FEATURES, 2], F32, align_bytes=64)
-            for h in range(2):
-                w_words = psum_acc.tile([P, 2, 2 * P], F32, name="w_words", tag="acc")
-                for u in range(2):
-                    for c in range(2):
-                        nc.tensor.transpose(
-                            w_words[:, u, c * P : (c + 1) * P],
-                            w_rows[:, 2 * h + c, :].bitcast(F32)[:, u : 2 * P : 2],
-                            ident[:],
-                        )
-                nc.vector.tensor_copy(
-                    out=w_grouped[:, h * 2 * P : (h + 1) * 2 * P, :],
-                    in_=w_words[:].rearrange("p u o -> p o u"),
-                )
+        def transpose_weights(h):
+            w_words = psum_acc.tile([P, 2, 2 * P], F32, name="w_words", tag="acc")
+            for u in range(2):
+                for c in range(2):
+                    nc.tensor.transpose(
+                        w_words[:, u, c * P : (c + 1) * P],
+                        w_rows[:, 2 * h + c, :].bitcast(F32)[:, u : 2 * P : 2],
+                        ident[:],
+                    )
+            return w_words
+
+        def group_weights(h, w_words):
+            nc.vector.tensor_copy(
+                out=w_grouped[:, h * 2 * P : (h + 1) * 2 * P, :],
+                in_=w_words[:].rearrange("p u o -> p o u"),
+            )
+
+        def quantise_weights():
             nc.vector.quantize_mx(
                 out=w_codes[:].bitcast(FP8X4),
                 scales=w_scales[:],
                 in_=w_grouped[:].rearrange("p o u -> p (o u)").bitcast(BF16),
             )
 
+        batches = [[0], [1]] + [[g, g + 1] for g in range(2, groups, 2)]
+        batch_of = {g: batch for batch in batches for g in batch}
+        mean_sq_of = {}
         rms_of = {}
-        inv_all_of = {}
+        inv_of = {}
+        factor_of = {}
+        factor_t_of = {}
         x_words_of = {}
         silu_of = {}
-        y_planes_of = {}
         y_grouped_of = {}
         y_codes_of = {}
         y_scales_of = {}
         acc_of = {}
+        result_of = {}
 
-        def root_mean_squares(g):
-            squares = work.tile([P, TILES, FEATURES], BF16, name="squares")
-            mean_sq = stats.tile([P, TILES], F32, name="mean_sq")
-            for j in range(TILES):
-                if g < VECTOR_SUMS:
-                    nc.vector.scalar_tensor_tensor(
-                        out=squares[:, j, :],
-                        in0=x_tiles[g][:, j, :],
-                        scalar=1.0 / FEATURES,
-                        in1=x_tiles[g][:, j, :],
-                        op0=ALU.mult,
-                        op1=ALU.mult,
-                        accum_out=mean_sq[:, j : j + 1],
-                    )
-                else:
-                    nc.scalar.activation(
-                        out=squares[:, j, :],
-                        in_=x_tiles[g][:, j, :],
-                        func=ACT.Square,
-                        scale=1.0 / math.sqrt(FEATURES),
-                        accum_out=mean_sq[:, j : j + 1],
-                    )
-            rms = stats.tile([P, TILES], F32, name="rms")
-            nc.gpsimd.tensor_tensor(out=rms[:], in0=mean_sq[:], in1=half[:], op=ALU.pow)
-            nc.gpsimd.tensor_scalar(out=rms[:], in0=rms[:], scalar1=EPS, scalar2=1.0, op0=ALU.add, op1=ALU.mult)
-            rms_of[g] = rms
+        def column(g, j):
+            return batch_of[g].index(g) * TILES + j
 
-        def spread_inverse_rms(g):
-            inv = stats.tile([P, TILES], F32, name="inv")
-            nc.vector.reciprocal(out=inv[:], in_=rms_of[g][:])
-            inv_all = psum_inv.tile([P, GROUP], F32, name="inv_all")
-            for j in range(TILES):
-                nc.tensor.transpose(
-                    inv_all[:, j * P : (j + 1) * P], inv[:, j : j + 1].to_broadcast([P, P]), ident[:]
-                )
-            inv_all_of[g] = inv_all
-
-        def transpose_x(g):
-            for u in range(2):
-                x_words = psum_words.tile([P, GROUP], F32, name="x_words")
-                for j in range(TILES):
-                    nc.tensor.transpose(
-                        x_words[:, j * P : (j + 1) * P],
-                        x_tiles[g][:, j, :].bitcast(F32)[:, u : 2 * P : 2],
-                        ident[:],
-                    )
-                x_words_of[(g, u)] = x_words
-
-        def gated(g):
-            silu = work.tile([P, PACK, GROUP], F32, name="silu")
-            for u in range(2):
-                pairs = x_words_of[(g, u)][:].bitcast(BF16).rearrange("p (m e) -> p m e", e=2)
-                for e in range(2):
-                    t = 2 * u + e
-                    nc.scalar.activation(
-                        out=silu[:, t, :], in_=pairs[:, :, e], func=ACT.Silu, scale=gate[:, t : t + 1]
-                    )
-            silu_of[g] = silu
-
-        def normed(g):
-            y_planes = work.tile([P, PACK, GROUP], BF16, name="y_planes")
-            for t in range(PACK):
+        def squares(g, j):
+            first = batch_of[g][0]
+            if column(g, j) == 0:
+                mean_sq_of[first] = stats.tile([P, len(batch_of[g]) * TILES], F32, name="mean_sq")
+            mean_sq = mean_sq_of[first][:, column(g, j) : column(g, j) + 1]
+            if (g, j) in VECTOR_SUMS:
+                scratch = work.tile([P, FEATURES], BF16, name="v_scratch")
                 nc.vector.scalar_tensor_tensor(
-                    out=y_planes[:, t, :],
-                    in0=silu_of[g][:, t, :],
-                    scalar=gain[:, t : t + 1],
-                    in1=inv_all_of[g][:],
+                    out=scratch[:],
+                    in0=x_tiles[g][:, j, :],
+                    scalar=1.0 / FEATURES,
+                    in1=x_tiles[g][:, j, :],
                     op0=ALU.mult,
                     op1=ALU.mult,
+                    accum_out=mean_sq,
                 )
-            y_planes_of[g] = y_planes
+            else:
+                scratch = work.tile([P, FEATURES], BF16, name="s_scratch")
+                nc.scalar.activation(
+                    out=scratch[:],
+                    in_=x_tiles[g][:, j, :],
+                    func=ACT.Square,
+                    scale=1.0 / math.sqrt(FEATURES),
+                    accum_out=mean_sq,
+                )
 
-        def regroup(g):
-            y_grouped = single.tile([P, GROUP, PACK], BF16, name="y_grouped", align_bytes=64)
+        def root(g):
+            if g == batch_of[g][0]:
+                width = len(batch_of[g]) * TILES
+                rms = stats.tile([P, width], F32, name="rms")
+                nc.gpsimd.tensor_tensor(out=rms[:], in0=mean_sq_of[g][:], in1=half[:, 0:width], op=ALU.pow)
+                nc.gpsimd.tensor_scalar(out=rms[:], in0=rms[:], scalar1=EPS, scalar2=1.0, op0=ALU.add, op1=ALU.mult)
+                rms_of[g] = rms
+
+        def inverse(g):
+            if g == batch_of[g][0]:
+                inv = stats.tile([P, len(batch_of[g]) * TILES], F32, name="inv")
+                nc.vector.reciprocal(out=inv[:], in_=rms_of[g][:])
+                inv_of[g] = inv
+
+        def factor(g, j):
+            f = factors.tile([P, PACK, P], F32, name="factor")
             nc.gpsimd.tensor_scalar(
-                out=y_grouped[:],
-                in0=y_planes_of[g][:].rearrange("p t m -> p m t"),
-                scalar1=1.0,
+                out=f[:],
+                in0=gain_row[:],
+                scalar1=inv_of[batch_of[g][0]][:, column(g, j) : column(g, j) + 1],
                 scalar2=0.0,
                 op0=ALU.mult,
                 op1=ALU.add,
             )
-            y_grouped_of[g] = y_grouped
+            factor_of[(g, j)] = f
 
-        def quantise(g):
-            y_codes = work.tile([P, GROUP], U32, name="y_codes", align_bytes=64)
-            y_scales = work.tile([P, GROUP], U8, name="y_scales", align_bytes=64)
-            nc.vector.quantize_mx(
-                out=y_codes[:].bitcast(FP8X4),
-                scales=y_scales[:],
-                in_=y_grouped_of[g][:].rearrange("p m t -> p (m t)"),
-            )
-            y_codes_of[g] = y_codes
-            y_scales_of[g] = y_scales
+        def transpose_factor(g, j):
+            factor_t = psum_factor.tile([P, PACK, P], F32, name="factor_t")
+            for t in range(PACK):
+                nc.tensor.transpose(factor_t[:, t, :], factor_of[(g, j)][:, t, :], ident[:])
+            factor_t_of[(g, j)] = factor_t
 
-        def multiply(g):
+        def transpose_x(g, u):
+            x_words = psum_words.tile([P, GROUP], F32, name="x_words")
             for j in range(TILES):
+                nc.tensor.transpose(
+                    x_words[:, j * P : (j + 1) * P],
+                    x_tiles[g][:, j, :].bitcast(F32)[:, u : 2 * P : 2],
+                    ident[:],
+                )
+            x_words_of[(g, u)] = x_words
+
+        def gated(g, u):
+            if u == 0:
+                silu_of[g] = work.tile([P, PACK, GROUP], F32, name="silu")
+            pairs = x_words_of[(g, u)][:].bitcast(BF16).rearrange("p (m e) -> p m e", e=2)
+            for e in range(2):
+                t = 2 * u + e
+                nc.scalar.activation(
+                    out=silu_of[g][:, t, :], in_=pairs[:, :, e], func=ACT.Silu, scale=gate[:, t : t + 1]
+                )
+
+        def normed(g, j):
+            if j == 0:
+                y_grouped_of[g] = work.tile([P, GROUP, PACK], BF16, name="y_grouped", align_bytes=64)
+            cols = slice(j * P, (j + 1) * P)
+            nc.vector.tensor_tensor(
+                out=y_grouped_of[g][:, cols, :].rearrange("p (c i) t -> p c t i", i=RUN),
+                in0=silu_of[g][:, :, cols].rearrange("p t (c i) -> p c t i", i=RUN),
+                in1=factor_t_of[(g, j)][:].rearrange("p t (c i) -> p c t i", i=RUN),
+                op=ALU.mult,
+            )
+
+        def quantise(g, first, count):
+            if first == 0:
+                y_codes_of[g] = work.tile([P, GROUP], U32, name="y_codes", align_bytes=64)
+                y_scales_of[g] = work.tile([P, GROUP], U8, name="y_scales", align_bytes=64)
+            cols = slice(first * P, (first + count) * P)
+            nc.vector.quantize_mx(
+                out=y_codes_of[g][:, cols].bitcast(FP8X4),
+                scales=y_scales_of[g][:, cols],
+                in_=y_grouped_of[g][:, cols, :].rearrange("p m t -> p (m t)"),
+            )
+
+        def multiply(g, first):
+            for j in range(first, first + 2):
                 acc = psum_acc.tile([P, OUT_FEATURES], F32, name="acc")
                 nc.tensor.matmul_mx(
                     out=acc[:],
@@ -226,25 +251,89 @@ def tile_normlocalattention_pb_t_kernel(tc, attn_out, norm_scale, norm_gate, w_o
                 )
                 acc_of[(g, j)] = acc
 
-        def add_bias_and_store(g):
-            result = results.tile([P, TILES, OUT_FEATURES], F32, name="result")
-            for j in range(TILES):
-                nc.vector.tensor_tensor(out=result[:, j, :], in0=acc_of[(g, j)][:], in1=bias[:], op=ALU.add)
-                nc.sync.dma_start(out=rows_of_group(out_rows, g)[:, j, :], in_=result[:, j, :])
+        def add_bias_and_store(g, j):
+            if j == 0:
+                result_of[g] = results.tile([P, TILES, OUT_FEATURES], F32, name="result")
+            nc.vector.tensor_tensor(
+                out=result_of[g][:, j, :],
+                in0=acc_of[(g, j)][:],
+                in1=bias_row[:].rearrange("p q t -> p (q t)"),
+                op=ALU.add,
+            )
+            nc.sync.dma_start(out=rows_of_group(out_rows, g)[:, j, :], in_=result_of[g][:, j, :])
 
-        def run(stage, g):
+        def run(stage, g, *rest):
             if 0 <= g < groups:
-                stage(g)
+                stage(g, *rest)
 
-        for step in range(-2, groups + 2):
-            run(gated, step + 1)
-            run(transpose_x, step + 2)
-            run(root_mean_squares, step + 2)
-            run(normed, step)
-            run(spread_inverse_rms, step + 1)
-            if step == 0:
-                prepare_weights()
-            run(quantise, step - 1)
-            run(multiply, step - 1)
-            run(add_bias_and_store, step - 2)
-            run(regroup, step)
+        transpose_x(0, 0)
+        transpose_x(0, 1)
+        for j in range(TILES):
+            squares(0, j)
+        nc.vector.reciprocal(out=gain[:], in_=gate[:])
+        nc.vector.tensor_mul(out=gain[:], in0=gain[:], in1=scale_bf[:])
+        nc.vector.tensor_copy(out=bias[:], in_=bias_bf[:])
+        root(0)
+        squares(1, 0)
+        gain_rows = spread(gain)
+        nc.vector.tensor_copy(out=gain_row[:], in_=gain_rows[:])
+        inverse(0)
+        factor(0, 0)
+        factor(0, 1)
+        for j in range(1, TILES):
+            squares(1, j)
+        root(1)
+        factor(0, 2)
+        factor(0, 3)
+        gated(0, 0)
+        gated(0, 1)
+        bias_rows = spread(bias)
+        transpose_factor(0, 0)
+        w_words = [transpose_weights(0)]
+        transpose_factor(0, 1)
+        transpose_x(1, 0)
+        transpose_x(1, 1)
+        for j in range(TILES):
+            squares(2, j)
+
+        for g in range(groups + 1):
+            last = g == groups - 1
+            for j in range(TILES):
+                run(squares, g + 3, j)
+            run(multiply, g - 1, 0)
+            run(normed, g, 0)
+            run(normed, g, 1)
+            run(inverse, g + 1)
+            run(factor, g + 1, 0)
+            run(factor, g + 1, 1)
+            run(transpose_factor, g, 2)
+            run(transpose_factor, g, 3)
+            run(multiply, g - 1, 2)
+            run(gated, g + 1, 0)
+            run(transpose_x, g + 2, 0)
+            if g == 0:
+                group_weights(0, w_words[0])
+                w_words.append(transpose_weights(1))
+            run(add_bias_and_store, g - 1, 0)
+            if last:
+                quantise(g, 0, 2)
+            run(normed, g, 2)
+            run(transpose_factor, g + 1, 0)
+            run(add_bias_and_store, g - 1, 1)
+            run(normed, g, 3)
+            run(gated, g + 1, 1)
+            run(transpose_x, g + 2, 1)
+            run(transpose_factor, g + 1, 1)
+            run(root, g + 2)
+            run(factor, g + 1, 2)
+            run(factor, g + 1, 3)
+            run(add_bias_and_store, g - 1, 2)
+            run(add_bias_and_store, g - 1, 3)
+            if g == 0:
+                group_weights(1, w_words[1])
+                nc.vector.tensor_copy(out=bias_row[:], in_=bias_rows[:].rearrange("p t q -> p q t"))
+                quantise_weights()
+            if last:
+                quantise(g, 2, 2)
+            else:
+                run(quantise, g, 0, TILES)

@@ -20,8 +20,8 @@ FEATURES = P * PACK
 OUT_FEATURES = 512
 TILES = 4
 GROUP = TILES * P
-RUN = 4
-VECTOR_SUMS = [(0, 0), (0, 1), (1, 0), (1, 1), (1, 2), (1, 3)]
+RUN = 2
+VECTOR_SUMS = [(0, 0), (0, 1), (1, 0), (1, 1)]
 EPS = 1e-8
 GATE_FLOOR = 2.0**-64
 
@@ -41,10 +41,9 @@ def tile_normlocalattention_pb_t_kernel(tc, attn_out, norm_scale, norm_gate, w_o
         x_pool = stack.enter_context(tc.tile_pool(name="x", bufs=1))
         stats = stack.enter_context(tc.tile_pool(name="stats", bufs=4))
         work = stack.enter_context(tc.tile_pool(name="work", bufs=3))
-        factors = stack.enter_context(tc.tile_pool(name="factors", bufs=2 * TILES))
         results = stack.enter_context(tc.tile_pool(name="results", bufs=3))
         psum_words = stack.enter_context(tc.psum_pool(name="psum_words", bufs=2))
-        psum_factor = stack.enter_context(tc.psum_pool(name="psum_factor", bufs=2))
+        psum_inv = stack.enter_context(tc.psum_pool(name="psum_inv", bufs=2))
         psum_acc = stack.enter_context(tc.psum_pool(name="psum_acc", bufs=TILES))
 
         gate_bf = const.tile([P, PACK], BF16)
@@ -82,14 +81,11 @@ def tile_normlocalattention_pb_t_kernel(tc, attn_out, norm_scale, norm_gate, w_o
         )
         nc.vector.tensor_add(out=gate[:], in0=gate_bf[:], in1=lift[:])
 
-        gain_row = const.tile([P, PACK, P], F32)
         bias_row = const.tile([P, P, PACK], F32)
 
-        def spread(column_tile):
-            rows = psum_acc.tile([P, PACK, P], F32, name="rows", tag="acc")
-            for t in range(PACK):
-                nc.tensor.transpose(rows[:, t, :], column_tile[:, t : t + 1].to_broadcast([P, P]), ident[:])
-            return rows
+        def spread(rows, columns):
+            for c in range(4):
+                nc.tensor.transpose(rows[:, c, :], columns[:, c : c + 1].to_broadcast([P, P]), ident[:])
 
         w_grouped = const.tile([P, OUT_FEATURES, 2], F32, align_bytes=64)
         w_codes = const.tile([P, OUT_FEATURES], U32, align_bytes=64)
@@ -119,15 +115,15 @@ def tile_normlocalattention_pb_t_kernel(tc, attn_out, norm_scale, norm_gate, w_o
                 in_=w_grouped[:].rearrange("p o u -> p (o u)").bitcast(BF16),
             )
 
-        batches = [[0], [1]] + [[g, g + 1] for g in range(2, groups, 2)]
+        batches = [[0], [1], [2], [3]] + [[g, g + 1] for g in range(4, groups, 2)]
         batch_of = {g: batch for batch in batches for g in batch}
         mean_sq_of = {}
         rms_of = {}
         inv_of = {}
-        factor_of = {}
-        factor_t_of = {}
+        inv_all_of = {}
         x_words_of = {}
         silu_of = {}
+        gained_of = {}
         y_grouped_of = {}
         y_codes_of = {}
         y_scales_of = {}
@@ -177,23 +173,11 @@ def tile_normlocalattention_pb_t_kernel(tc, attn_out, norm_scale, norm_gate, w_o
                 nc.vector.reciprocal(out=inv[:], in_=rms_of[g][:])
                 inv_of[g] = inv
 
-        def factor(g, j):
-            f = factors.tile([P, PACK, P], F32, name="factor")
-            nc.gpsimd.tensor_scalar(
-                out=f[:],
-                in0=gain_row[:],
-                scalar1=inv_of[batch_of[g][0]][:, column(g, j) : column(g, j) + 1],
-                scalar2=0.0,
-                op0=ALU.mult,
-                op1=ALU.add,
-            )
-            factor_of[(g, j)] = f
-
-        def transpose_factor(g, j):
-            factor_t = psum_factor.tile([P, PACK, P], F32, name="factor_t")
-            for t in range(PACK):
-                nc.tensor.transpose(factor_t[:, t, :], factor_of[(g, j)][:, t, :], ident[:])
-            factor_t_of[(g, j)] = factor_t
+        def spread_inverse(g):
+            inv_all = psum_inv.tile([P, TILES, P], F32, name="inv_all")
+            first = column(g, 0)
+            spread(inv_all, inv_of[batch_of[g][0]][:, first : first + TILES])
+            inv_all_of[g] = inv_all
 
         def transpose_x(g, u):
             x_words = psum_words.tile([P, GROUP], F32, name="x_words")
@@ -215,14 +199,30 @@ def tile_normlocalattention_pb_t_kernel(tc, attn_out, norm_scale, norm_gate, w_o
                     out=silu_of[g][:, t, :], in_=pairs[:, :, e], func=ACT.Silu, scale=gate[:, t : t + 1]
                 )
 
-        def normed(g, j):
-            if j == 0:
+        def gained(g):
+            gained_of[g] = work.tile([P, PACK, GROUP], F32, name="gained")
+            engine = nc.vector if g == 0 else nc.gpsimd
+            for t in range(PACK):
+                engine.tensor_scalar(
+                    out=gained_of[g][:, t, :],
+                    in0=silu_of[g][:, t, :],
+                    scalar1=gain[:, t : t + 1],
+                    scalar2=0.0,
+                    op0=ALU.mult,
+                    op1=ALU.add,
+                )
+
+        def normed(g, first, count):
+            if first == 0:
                 y_grouped_of[g] = work.tile([P, GROUP, PACK], BF16, name="y_grouped", align_bytes=64)
-            cols = slice(j * P, (j + 1) * P)
+            cols = slice(first * P, (first + count) * P)
+            inv = inv_all_of[g][:].rearrange("p j m -> p (j m)")[:, cols]
             nc.vector.tensor_tensor(
                 out=y_grouped_of[g][:, cols, :].rearrange("p (c i) t -> p c t i", i=RUN),
-                in0=silu_of[g][:, :, cols].rearrange("p t (c i) -> p c t i", i=RUN),
-                in1=factor_t_of[(g, j)][:].rearrange("p t (c i) -> p c t i", i=RUN),
+                in0=gained_of[g][:, :, cols].rearrange("p t (c i) -> p c t i", i=RUN),
+                in1=inv.rearrange("p (c i) -> p c i", i=RUN)
+                .unsqueeze(2)
+                .to_broadcast([P, count * P // RUN, PACK, RUN]),
                 op=ALU.mult,
             )
 
@@ -237,8 +237,8 @@ def tile_normlocalattention_pb_t_kernel(tc, attn_out, norm_scale, norm_gate, w_o
                 in_=y_grouped_of[g][:, cols, :].rearrange("p m t -> p (m t)"),
             )
 
-        def multiply(g, first):
-            for j in range(first, first + 2):
+        def multiply(g):
+            for j in range(TILES):
                 acc = psum_acc.tile([P, OUT_FEATURES], F32, name="acc")
                 nc.tensor.matmul_mx(
                     out=acc[:],
@@ -275,24 +275,22 @@ def tile_normlocalattention_pb_t_kernel(tc, attn_out, norm_scale, norm_gate, w_o
         nc.vector.tensor_copy(out=bias[:], in_=bias_bf[:])
         root(0)
         squares(1, 0)
-        gain_rows = spread(gain)
-        nc.vector.tensor_copy(out=gain_row[:], in_=gain_rows[:])
+        squares(1, 1)
         inverse(0)
-        factor(0, 0)
-        factor(0, 1)
-        for j in range(1, TILES):
-            squares(1, j)
-        root(1)
-        factor(0, 2)
-        factor(0, 3)
+        spread_inverse(0)
         gated(0, 0)
         gated(0, 1)
-        bias_rows = spread(bias)
-        transpose_factor(0, 0)
-        w_words = [transpose_weights(0)]
-        transpose_factor(0, 1)
+        gained(0)
+        squares(1, 2)
+        squares(1, 3)
+        root(1)
         transpose_x(1, 0)
         transpose_x(1, 1)
+        bias_rows = psum_acc.tile([P, PACK, P], F32, name="bias_rows", tag="acc")
+        spread(bias_rows, bias)
+        w_words = [transpose_weights(0), transpose_weights(1)]
+        gated(1, 0)
+        gated(1, 1)
         for j in range(TILES):
             squares(2, j)
 
@@ -300,39 +298,28 @@ def tile_normlocalattention_pb_t_kernel(tc, attn_out, norm_scale, norm_gate, w_o
             last = g == groups - 1
             for j in range(TILES):
                 run(squares, g + 3, j)
-            run(multiply, g - 1, 0)
-            run(normed, g, 0)
-            run(normed, g, 1)
+            run(multiply, g - 1)
+            run(normed, g, 0, 2)
             run(inverse, g + 1)
-            run(factor, g + 1, 0)
-            run(factor, g + 1, 1)
-            run(transpose_factor, g, 2)
-            run(transpose_factor, g, 3)
-            run(multiply, g - 1, 2)
-            run(gated, g + 1, 0)
+            run(gained, g + 1)
+            run(root, g + 2)
+            run(spread_inverse, g + 1)
             run(transpose_x, g + 2, 0)
+            run(transpose_x, g + 2, 1)
+            run(gated, g + 2, 0)
+            run(gated, g + 2, 1)
+            run(normed, g, 2, 2)
             if g == 0:
                 group_weights(0, w_words[0])
-                w_words.append(transpose_weights(1))
-            run(add_bias_and_store, g - 1, 0)
-            if last:
-                quantise(g, 0, 2)
-            run(normed, g, 2)
-            run(transpose_factor, g + 1, 0)
-            run(add_bias_and_store, g - 1, 1)
-            run(normed, g, 3)
-            run(gated, g + 1, 1)
-            run(transpose_x, g + 2, 1)
-            run(transpose_factor, g + 1, 1)
-            run(root, g + 2)
-            run(factor, g + 1, 2)
-            run(factor, g + 1, 3)
-            run(add_bias_and_store, g - 1, 2)
-            run(add_bias_and_store, g - 1, 3)
-            if g == 0:
                 group_weights(1, w_words[1])
                 nc.vector.tensor_copy(out=bias_row[:], in_=bias_rows[:].rearrange("p t q -> p q t"))
                 quantise_weights()
+            run(add_bias_and_store, g - 1, 0)
+            run(add_bias_and_store, g - 1, 1)
+            if last:
+                quantise(g, 0, 2)
+            run(add_bias_and_store, g - 1, 2)
+            run(add_bias_and_store, g - 1, 3)
             if last:
                 quantise(g, 2, 2)
             else:

@@ -115,7 +115,7 @@ def tile_normlocalattention_pb_t_kernel(tc, attn_out, norm_scale, norm_gate, w_o
                 in_=w_grouped[:].rearrange("p o u -> p (o u)").bitcast(BF16),
             )
 
-        batches = [[0], [1], [2], [3]] + [[g, g + 1] for g in range(4, groups, 2)]
+        batches = [[g] for g in range(groups)]
         batch_of = {g: batch for batch in batches for g in batch}
         mean_sq_of = {}
         rms_of = {}
@@ -262,6 +262,10 @@ def tile_normlocalattention_pb_t_kernel(tc, attn_out, norm_scale, norm_gate, w_o
             )
             nc.sync.dma_start(out=rows_of_group(out_rows, g)[:, j, :], in_=result_of[g][:, j, :])
 
+        def after_quantise(g):
+            mark = stats.tile([P, 1], U32, name="mark")
+            nc.gpsimd.tensor_copy(out=mark[:], in_=y_codes_of[g][:, 0:1])
+
         def run(stage, g, *rest):
             if 0 <= g < groups:
                 stage(g, *rest)
@@ -301,6 +305,8 @@ def tile_normlocalattention_pb_t_kernel(tc, attn_out, norm_scale, norm_gate, w_o
             run(multiply, g - 1)
             run(normed, g, 0, 2)
             run(inverse, g + 1)
+            if 0 <= g - 1 < groups - 2:
+                after_quantise(g - 1)
             run(gained, g + 1)
             run(root, g + 2)
             run(spread_inverse, g + 1)

from contextlib import ExitStack
import math

import concourse.mybir as mybir
from concourse.masks import make_identity

FLOPS = 2 * 8192 * 512 * 512

BF16 = mybir.dt.bfloat16
F32 = mybir.dt.float32
U32 = mybir.dt.uint32
U8 = mybir.dt.uint8
FP8X4 = mybir.dt.float8_e4m3fn_x4
ACT = mybir.ActivationFunctionType
ALU = mybir.AluOpType

P = 128
PACK = 4
FEATURES = P * PACK
OUT_FEATURES = 512
TILES = 4
GROUP = TILES * P
RUN = 2
VECTOR_SUMS = [(0, 0), (0, 1), (1, 0), (1, 1)]
EPS = 1e-8
GATE_FLOOR = 2.0**-64


def tile_normlocalattention_pb_t_kernel(tc, attn_out, norm_scale, norm_gate, w_o, b_o, out):
    nc = tc.nc
    x_rows = attn_out.flatten_outer_dims()
    out_rows = out.flatten_outer_dims()
    groups = x_rows.shape[0] // GROUP

    def rows_of_group(rows, g):
        return rows[g * GROUP : (g + 1) * GROUP, :].rearrange("(p j) k -> p j k", j=TILES)

    with ExitStack() as stack:
        stack.enter_context(tc.manual_schedule())
        const = stack.enter_context(tc.tile_pool(name="const", bufs=1))
        x_pool = stack.enter_context(tc.tile_pool(name="x", bufs=1))
        stats = stack.enter_context(tc.tile_pool(name="stats", bufs=4))
        work = stack.enter_context(tc.tile_pool(name="work", bufs=3))
        results = stack.enter_context(tc.tile_pool(name="results", bufs=3))
        psum_words = stack.enter_context(tc.psum_pool(name="psum_words", bufs=2))
        psum_inv = stack.enter_context(tc.psum_pool(name="psum_inv", bufs=2))
        psum_acc = stack.enter_context(tc.psum_pool(name="psum_acc", bufs=TILES))

        gate_bf = const.tile([P, PACK], BF16)
        scale_bf = const.tile([P, PACK], BF16)
        bias_bf = const.tile([P, PACK], BF16)
        nc.scalar.dma_start(out=gate_bf[:], in_=norm_gate.rearrange("(p t) -> p t", t=PACK))
        nc.scalar.dma_start(out=scale_bf[:], in_=norm_scale.rearrange("(p t) -> p t", t=PACK))
        nc.scalar.dma_start(out=bias_bf[:], in_=b_o.rearrange("(p t) -> p t", t=PACK))
        x_tiles = [x_pool.tile([P, TILES, FEATURES], BF16, name="x_tile_%d" % g) for g in range(groups)]
        w_rows = const.tile([P, OUT_FEATURES // P, FEATURES], BF16)
        for j in range(TILES):
            nc.sync.dma_start(out=x_tiles[0][:, j, :], in_=rows_of_group(x_rows, 0)[:, j, :])
        nc.sync.dma_start(out=x_tiles[1][:], in_=rows_of_group(x_rows, 1))
        nc.sync.dma_start(out=w_rows[:], in_=w_o.rearrange("(c p) k -> p c k", p=P))
        for g in range(2, groups):
            nc.sync.dma_start(out=x_tiles[g][:], in_=rows_of_group(x_rows, g))

        ident = const.tile([P, P], F32)
        make_identity(nc, ident[:])
        half = const.tile([P, 2 * TILES], F32)
        nc.vector.memset(half[:], 0.5)
        warm = const.tile([P, 1], F32)
        nc.scalar.activation(out=warm[:], in_=half[:, 0:1], func=ACT.Silu)

        gate = const.tile([P, PACK], F32)
        size = const.tile([P, PACK], F32)
        lift = const.tile([P, PACK], F32)
        gain = const.tile([P, PACK], F32)
        bias = const.tile([P, PACK], F32)
        nc.vector.scalar_tensor_tensor(
            out=size[:], in0=gate_bf[:], scalar=-1.0, in1=gate_bf[:], op0=ALU.mult, op1=ALU.max
        )
        nc.vector.tensor_scalar(
            out=lift[:], in0=size[:], scalar1=GATE_FLOOR, scalar2=GATE_FLOOR, op0=ALU.is_lt, op1=ALU.mult
        )
        nc.vector.tensor_add(out=gate[:], in0=gate_bf[:], in1=lift[:])

        bias_row = const.tile([P, P, PACK], F32)

        def spread(rows, columns):
            for c in range(4):
                nc.tensor.transpose(rows[:, c, :], columns[:, c : c + 1].to_broadcast([P, P]), ident[:])

        w_grouped = const.tile([P, OUT_FEATURES, 2], F32, align_bytes=64)
        w_codes = const.tile([P, OUT_FEATURES], U32, align_bytes=64)
        w_scales = const.tile([P, OUT_FEATURES], U8, align_bytes=64)

        def transpose_weights(h):
            w_words = psum_acc.tile([P, 2, 2 * P], F32, name="w_words", tag="acc")
            for u in range(2):
                for c in range(2):
                    nc.tensor.transpose(
                        w_words[:, u, c * P : (c + 1) * P],
                        w_rows[:, 2 * h + c, :].bitcast(F32)[:, u : 2 * P : 2],
                        ident[:],
                    )
            return w_words

        def group_weights(h, w_words):
            nc.vector.tensor_copy(
                out=w_grouped[:, h * 2 * P : (h + 1) * 2 * P, :],
                in_=w_words[:].rearrange("p u o -> p o u"),
            )

        def quantise_weights():
            nc.vector.quantize_mx(
                out=w_codes[:].bitcast(FP8X4),
                scales=w_scales[:],
                in_=w_grouped[:].rearrange("p o u -> p (o u)").bitcast(BF16),
            )

        batches = [[g] for g in range(groups)]
        batch_of = {g: batch for batch in batches for g in batch}
        mean_sq_of = {}
        rms_of = {}
        inv_of = {}
        inv_all_of = {}
        x_words_of = {}
        silu_of = {}
        gained_of = {}
        y_grouped_of = {}
        y_codes_of = {}
        y_scales_of = {}
        acc_of = {}
        result_of = {}

        def column(g, j):
            return batch_of[g].index(g) * TILES + j

        def squares(g, j):
            first = batch_of[g][0]
            if column(g, j) == 0:
                mean_sq_of[first] = stats.tile([P, len(batch_of[g]) * TILES], F32, name="mean_sq")
            mean_sq = mean_sq_of[first][:, column(g, j) : column(g, j) + 1]
            if (g, j) in VECTOR_SUMS:
                scratch = work.tile([P, FEATURES], BF16, name="v_scratch")
                nc.vector.scalar_tensor_tensor(
                    out=scratch[:],
                    in0=x_tiles[g][:, j, :],
                    scalar=1.0 / FEATURES,
                    in1=x_tiles[g][:, j, :],
                    op0=ALU.mult,
                    op1=ALU.mult,
                    accum_out=mean_sq,
                )
            else:
                scratch = work.tile([P, FEATURES], BF16, name="s_scratch")
                nc.scalar.activation(
                    out=scratch[:],
                    in_=x_tiles[g][:, j, :],
                    func=ACT.Square,
                    scale=1.0 / math.sqrt(FEATURES),
                    accum_out=mean_sq,
                )

        def root(g):
            if g == batch_of[g][0]:
                width = len(batch_of[g]) * TILES
                rms = stats.tile([P, width], F32, name="rms")
                nc.gpsimd.tensor_tensor(out=rms[:], in0=mean_sq_of[g][:], in1=half[:, 0:width], op=ALU.pow)
                nc.gpsimd.tensor_scalar(out=rms[:], in0=rms[:], scalar1=EPS, scalar2=1.0, op0=ALU.add, op1=ALU.mult)
                rms_of[g] = rms

        def inverse(g):
            if g == batch_of[g][0]:
                inv = stats.tile([P, len(batch_of[g]) * TILES], F32, name="inv")
                nc.vector.reciprocal(out=inv[:], in_=rms_of[g][:])
                inv_of[g] = inv

        def spread_inverse(g):
            inv_all = psum_inv.tile([P, TILES, P], F32, name="inv_all")
            first = column(g, 0)
            spread(inv_all, inv_of[batch_of[g][0]][:, first : first + TILES])
            inv_all_of[g] = inv_all

        def transpose_x(g, u):
            x_words = psum_words.tile([P, GROUP], F32, name="x_words")
            for j in range(TILES):
                nc.tensor.transpose(
                    x_words[:, j * P : (j + 1) * P],
                    x_tiles[g][:, j, :].bitcast(F32)[:, u : 2 * P : 2],
                    ident[:],
                )
            x_words_of[(g, u)] = x_words

        def gated(g, u):
            if u == 0:
                silu_of[g] = work.tile([P, PACK, GROUP], F32, name="silu")
            pairs = x_words_of[(g, u)][:].bitcast(BF16).rearrange("p (m e) -> p m e", e=2)
            for e in range(2):
                t = 2 * u + e
                nc.scalar.activation(
                    out=silu_of[g][:, t, :], in_=pairs[:, :, e], func=ACT.Silu, scale=gate[:, t : t + 1]
                )

        def gained(g):
            gained_of[g] = work.tile([P, PACK, GROUP], F32, name="gained")
            engine = nc.vector if g == 0 else nc.gpsimd
            for t in range(PACK):
                engine.tensor_scalar(
                    out=gained_of[g][:, t, :],
                    in0=silu_of[g][:, t, :],
                    scalar1=gain[:, t : t + 1],
                    scalar2=0.0,
                    op0=ALU.mult,
                    op1=ALU.add,
                )

        def normed(g, first, count):
            if first == 0:
                y_grouped_of[g] = work.tile([P, GROUP, PACK], BF16, name="y_grouped", align_bytes=64)
            cols = slice(first * P, (first + count) * P)
            inv = inv_all_of[g][:].rearrange("p j m -> p (j m)")[:, cols]
            nc.vector.tensor_tensor(
                out=y_grouped_of[g][:, cols, :].rearrange("p (c i) t -> p c t i", i=RUN),
                in0=gained_of[g][:, :, cols].rearrange("p t (c i) -> p c t i", i=RUN),
                in1=inv.rearrange("p (c i) -> p c i", i=RUN)
                .unsqueeze(2)
                .to_broadcast([P, count * P // RUN, PACK, RUN]),
                op=ALU.mult,
            )

        def quantise(g, first, count):
            if first == 0:
                y_codes_of[g] = work.tile([P, GROUP], U32, name="y_codes", align_bytes=64)
                y_scales_of[g] = work.tile([P, GROUP], U8, name="y_scales", align_bytes=64)
            cols = slice(first * P, (first + count) * P)
            nc.vector.quantize_mx(
                out=y_codes_of[g][:, cols].bitcast(FP8X4),
                scales=y_scales_of[g][:, cols],
                in_=y_grouped_of[g][:, cols, :].rearrange("p m t -> p (m t)"),
            )

        def multiply(g):
            for j in range(TILES):
                acc = psum_acc.tile([P, OUT_FEATURES], F32, name="acc")
                nc.tensor.matmul_mx(
                    out=acc[:],
                    lhsT=y_codes_of[g][:, j * P : (j + 1) * P].bitcast(FP8X4),
                    lhsT_scale=y_scales_of[g][:, j * P : (j + 1) * P],
                    rhs=w_codes[:].bitcast(FP8X4),
                    rhs_scale=w_scales[:],
                    start=True,
                    stop=True,
                )
                acc_of[(g, j)] = acc

        def add_bias_and_store(g, j):
            if j == 0:
                result_of[g] = results.tile([P, TILES, OUT_FEATURES], F32, name="result")
            nc.vector.tensor_tensor(
                out=result_of[g][:, j, :],
                in0=acc_of[(g, j)][:],
                in1=bias_row[:].rearrange("p q t -> p (q t)"),
                op=ALU.add,
            )
            nc.sync.dma_start(out=rows_of_group(out_rows, g)[:, j, :], in_=result_of[g][:, j, :])

        def after_quantise(g):
            mark = stats.tile([P, 1], U32, name="mark")
            nc.gpsimd.tensor_copy(out=mark[:], in_=y_codes_of[g][:, 0:1])

        def run(stage, g, *rest):
            if 0 <= g < groups:
                stage(g, *rest)

        transpose_x(0, 0)
        transpose_x(0, 1)
        for j in range(TILES):
            squares(0, j)
        nc.vector.reciprocal(out=gain[:], in_=gate[:])
        nc.vector.tensor_mul(out=gain[:], in0=gain[:], in1=scale_bf[:])
        nc.vector.tensor_copy(out=bias[:], in_=bias_bf[:])
        root(0)
        squares(1, 0)
        squares(1, 1)
        inverse(0)
        spread_inverse(0)
        gated(0, 0)
        gated(0, 1)
        gained(0)
        squares(1, 2)
        squares(1, 3)
        root(1)
        transpose_x(1, 0)
        transpose_x(1, 1)
        bias_rows = psum_acc.tile([P, PACK, P], F32, name="bias_rows", tag="acc")
        spread(bias_rows, bias)
        w_words = [transpose_weights(0), transpose_weights(1)]
        gated(1, 0)
        gated(1, 1)
        for j in range(TILES):
            squares(2, j)

        for g in range(groups + 1):
            last = g == groups - 1
            for j in range(TILES):
                run(squares, g + 3, j)
            run(multiply, g - 1)
            run(normed, g, 0, 2)
            run(inverse, g + 1)
            if 0 <= g - 1 < groups - 2:
                after_quantise(g - 1)
            run(gained, g + 1)
            run(root, g + 2)
            run(spread_inverse, g + 1)
            run(transpose_x, g + 2, 0)
            run(transpose_x, g + 2, 1)
            run(gated, g + 2, 0)
            run(gated, g + 2, 1)
            run(normed, g, 2, 2)
            if g == 0:
                group_weights(0, w_words[0])
                group_weights(1, w_words[1])
                nc.vector.tensor_copy(out=bias_row[:], in_=bias_rows[:].rearrange("p t q -> p q t"))
                quantise_weights()
            run(add_bias_and_store, g - 1, 0)
            run(add_bias_and_store, g - 1, 1)
            if last:
                quantise(g, 0, 2)
            run(add_bias_and_store, g - 1, 2)
            run(add_bias_and_store, g - 1, 3)
            if last:
                quantise(g, 2, 2)
            else:
                run(quantise, g, 0, TILES)
